import numpy as np
import ml_dtypes


def mxq(x, axis, fmt="e4m3"):
    dtype, down = {"e4m3": (ml_dtypes.float8_e4m3fn, 7), "e5m2": (ml_dtypes.float8_e5m2, 14)}[fmt]
    v = np.moveaxis(np.asarray(x, np.float32).astype(ml_dtypes.bfloat16).astype(np.float64), axis, -1)
    blocks = v.reshape(v.shape[:-1] + (-1, 32))
    amax = np.abs(blocks).max(-1, keepdims=True)
    byte = np.maximum(np.where(amax > 0, np.frexp(amax)[1] - 1 + 127, 0) - down, 1)
    scale = np.exp2(byte - 127.0)
    codes = (blocks / scale).astype(np.float32).astype(dtype).astype(np.float64)
    return np.moveaxis((codes * scale).reshape(v.shape), -1, axis)


WIDE = False


def mx_kscale(k):
    if not WIDE:
        return np.ones(k)
    levels = np.array([10, -10, 5, -5, 0])
    a = np.random.permutation(np.resize(levels, k // 512 * 4)).reshape(k // 512, 4)
    idx = np.arange(k)
    return np.exp2(a[idx // 512, idx % 128 // 32])


BF16 = ml_dtypes.bfloat16


def bf(x):
    return np.asarray(x, np.float32).astype(BF16)


def f64(x):
    return np.asarray(x).astype(np.float64)


T, K, D = 512, 16384, 256
ACTIVE = 128.0


def setup_inputs():
    s = mx_kscale(K)
    allow = s <= max(s.min(), s.max() * 2.0 ** -18)
    p = np.maximum(np.random.uniform(-0.15, 1.0, (T, 1)), 0.0) * ACTIVE / K
    on = (np.random.uniform(size=(T, K)) < p) & allow[None, :]
    flags = 0.5 * np.random.uniform(size=(T, K)) + 0.5 * on
    w = np.random.standard_normal((K, D)) * (s / s.min())[:, None]
    return {"flags_matrix": bf(flags), "emb_weight": bf(w)}


def reference(flags_matrix, emb_weight):
    mask = (f64(flags_matrix) > 0.5).astype(np.float64)
    counts = np.sum(mask, axis=1, keepdims=True)
    sums = mxq(mask, 1, "e4m3") @ mxq(f64(emb_weight), 0, "e4m3")
    return np.where(counts > 0, sums / np.maximum(counts, 1.0), 0.0)

@@ -1,0 +1,210 @@
+from contextlib import ExitStack
+
+import concourse.mybir as mybir
+from concourse.masks import make_identity
+
+BF16 = mybir.dt.bfloat16
+F32 = mybir.dt.float32
+U32 = mybir.dt.uint32
+U8 = mybir.dt.uint8
+FP8X4 = mybir.dt.float8_e4m3fn_x4
+ALU = mybir.AluOpType
+AX = mybir.AxisListType
+ACT = mybir.ActivationFunctionType
+
+T, K, D = 512, 16384, 256
+FLOPS = 2 * T * K * D
+
+P = 128
+PACK = 4
+K_PASS = P * PACK
+PASSES = K // K_PASS
+ROW_TILES = T // P
+
+UNIT_K = 4096
+UNIT_PASSES = UNIT_K // K_PASS
+UNITS = ROW_TILES * (K // UNIT_K)
+BANK_PASSES = 2
+UNIT_BANKS = UNIT_PASSES // BANK_PASSES
+
+PIECE_PASSES = 4
+PIECES = PASSES // PIECE_PASSES
+VECTOR_PIECES = 2
+
+FIRST_SLOT = -2
+LOAD_LEAD = 6
+COUNTS_SLOT = UNITS - 1 + FIRST_SLOT
+
+
+def piece_slot(h):
+    if h < VECTOR_PIECES:
+        return FIRST_SLOT + h
+    return 2 * h - 5
+
+
+def tile_flagbagencoder_k_kernel(tc, flags_matrix, emb_weight, out):
+    nc = tc.nc
+    with ExitStack() as ctx:
+        consts = ctx.enter_context(tc.tile_pool(name="consts", bufs=1))
+        flag_pool = ctx.enter_context(tc.tile_pool(name="flags", bufs=LOAD_LEAD + 2))
+        wraw_pool = ctx.enter_context(tc.tile_pool(name="wraw", bufs=5))
+        wgrp_pool = ctx.enter_context(tc.tile_pool(name="wgrp", bufs=2))
+        grouped_pool = ctx.enter_context(tc.tile_pool(name="grouped", bufs=2))
+        codes_pool = ctx.enter_context(tc.tile_pool(name="codes", bufs=2))
+        result_pool = ctx.enter_context(tc.tile_pool(name="result", bufs=2))
+        psum_words = ctx.enter_context(tc.psum_pool(name="words", bufs=UNIT_BANKS))
+        psum_sums = ctx.enter_context(tc.psum_pool(name="sums", bufs=1))
+
+        flags_view = flags_matrix.rearrange("(a p) (c k) -> c a p k", p=P, k=UNIT_K)
+        weight_view = emb_weight.rearrange("(s u p e) d -> p s u e d", u=2, p=P, e=2)
+
+        identity = consts.tile([P, P], F32)
+        make_identity(nc, identity[:])
+
+        weight_codes = consts.tile([P, PASSES, D], U32, align_bytes=64)
+        weight_scales = consts.tile([P, PASSES, D], U8, align_bytes=64)
+        count_parts = consts.tile([P, UNITS], F32)
+        counts = consts.tile([P, ROW_TILES], F32)
+        inverse_counts = consts.tile([P, ROW_TILES], F32)
+        sums = [psum_sums.tile([P, D], F32, name="sums%d" % a) for a in range(ROW_TILES)]
+
+        flag_tiles = {}
+        wraw_tiles = {}
+        wgrp_tiles = {}
+        grouped_tiles = {}
+        mask_codes = {}
+        mask_scales = {}
+
+        def load_flags(i):
+            c, a = divmod(i, ROW_TILES)
+            flag_tiles[i] = flag_pool.tile([P, UNIT_K], BF16, name="flags")
+            nc.sync.dma_start(out=flag_tiles[i][:], in_=flags_view[c, a])
+
+        def load_weights(h):
+            wraw_tiles[h] = wraw_pool.tile([P, PIECE_PASSES, PACK, D], BF16, name="wraw")
+            nc.sync.dma_start(
+                out=wraw_tiles[h][:].rearrange("p s (u e) d -> p s u e d", u=2),
+                in_=weight_view[:, h * PIECE_PASSES : (h + 1) * PIECE_PASSES],
+            )
+
+        def threshold_and_count(i):
+            nc.vector.tensor_scalar(
+                out=flag_tiles[i][:],
+                in0=flag_tiles[i][:],
+                scalar1=0.5,
+                scalar2=None,
+                op0=ALU.is_gt,
+                op1=ALU.add,
+                accum_out=count_parts[:, i : i + 1],
+            )
+
+        def transpose_and_group(i):
+            words = flag_tiles[i][:].bitcast(F32)
+            grouped_tiles[i] = grouped_pool.tile([P, UNIT_K], BF16, name="grouped", align_bytes=64)
+            grouped_words = (
+                grouped_tiles[i][:].bitcast(F32).rearrange("p (g t u) -> p g t u", g=UNIT_PASSES, u=2)
+            )
+            for b in range(UNIT_BANKS):
+                bank = psum_words.tile([P, BANK_PASSES, 2, P], F32, name="bank")
+                for g in range(BANK_PASSES):
+                    for u in range(2):
+                        first = ((b * BANK_PASSES + g) * 2 + u) * P
+                        nc.tensor.transpose(bank[:, g, u, :], words[:, first : first + P], identity[:])
+                nc.scalar.copy(
+                    out=grouped_words[:, b * BANK_PASSES : (b + 1) * BANK_PASSES],
+                    in_=bank[:].rearrange("p g u t -> p g t u"),
+                )
+
+        def quantise_mask(i):
+            mask_codes[i] = codes_pool.tile([P, UNIT_K // PACK], U32, name="mcodes", align_bytes=64)
+            mask_scales[i] = codes_pool.tile([P, UNIT_K // PACK], U8, name="mscales", align_bytes=64)
+            nc.vector.quantize_mx(
+                out=mask_codes[i][:].bitcast(FP8X4), scales=mask_scales[i][:], in_=grouped_tiles[i][:]
+            )
+
+        def regroup_weights(copy, h, s):
+            if s == 0:
+                wgrp_tiles[h] = wgrp_pool.tile([P, PIECE_PASSES, D, PACK], BF16, name="wgrp", align_bytes=64)
+            copy(
+                out=wgrp_tiles[h][:, s].rearrange("p (c i) j -> p c j i", i=4),
+                in_=wraw_tiles[h][:, s].rearrange("p j (c i) -> p c j i", i=4),
+            )
+
+        def quantise_weights(h):
+            piece = slice(h * PIECE_PASSES, (h + 1) * PIECE_PASSES)
+            nc.vector.quantize_mx(
+                out=weight_codes[:, piece, :].rearrange("p s d -> p (s d)").bitcast(FP8X4),
+                scales=weight_scales[:, piece, :].rearrange("p s d -> p (s d)"),
+                in_=wgrp_tiles[h][:].rearrange("p s d j -> p (s d j)"),
+            )
+
+        def multiply(i):
+            c, a = divmod(i, ROW_TILES)
+            for g in range(UNIT_PASSES):
+                s = c * UNIT_PASSES + g
+                rows = slice(g * P, (g + 1) * P)
+                nc.tensor.matmul_mx(
+                    out=sums[a][:],
+                    lhsT=mask_codes[i][:, rows].bitcast(FP8X4),
+                    lhsT_scale=mask_scales[i][:, rows],
+                    rhs=weight_codes[:, s, :].bitcast(FP8X4),
+                    rhs_scale=weight_scales[:, s, :],
+                    start=(s == 0),
+                    stop=(s == PASSES - 1),
+                )
+
+        def invert_counts():
+            nc.vector.tensor_reduce(
+                out=counts[:],
+                in_=count_parts[:].rearrange("p (c a) -> p a c", a=ROW_TILES),
+                axis=AX.X,
+                op=ALU.add,
+            )
+            nc.vector.tensor_scalar_max(out=counts[:], in0=counts[:], scalar1=1.0)
+            nc.vector.reciprocal(out=inverse_counts[:], in_=counts[:])
+
+        def divide_and_store(a):
+            result = result_pool.tile([P, D], F32, name="result")
+            nc.scalar.activation(out=result[:], in_=sums[a][:], func=ACT.Copy, scale=inverse_counts[:, a : a + 1])
+            nc.sync.dma_start(out=out[a * P : (a + 1) * P, :], in_=result[:])
+
+        for slot in range(FIRST_SLOT - LOAD_LEAD, UNITS):
+            ahead = slot + LOAD_LEAD
+            if 0 <= ahead - FIRST_SLOT < UNITS:
+                load_flags(ahead - FIRST_SLOT)
+            for h in range(PIECES):
+                if piece_slot(h) == ahead:
+                    load_weights(h)
+            if slot < FIRST_SLOT:
+                continue
+
+            if slot >= 0:
+                quantise_mask(slot)
+            if slot - FIRST_SLOT < UNITS:
+                threshold_and_count(slot - FIRST_SLOT)
+            if slot == COUNTS_SLOT:
+                invert_counts()
+            for h in range(PIECES):
+                if h < VECTOR_PIECES and piece_slot(h) + 1 == slot:
+                    quantise_weights(h)
+                if h >= VECTOR_PIECES and piece_slot(h) + 2 == slot:
+                    quantise_weights(h)
+            for h in range(VECTOR_PIECES):
+                if piece_slot(h) == slot:
+                    for s in range(PIECE_PASSES):
+                        regroup_weights(nc.vector.tensor_copy, h, s)
+
+            scalar_piece, half = divmod(slot + 5, 2)
+            has_piece = VECTOR_PIECES <= scalar_piece < PIECES
+            if has_piece:
+                regroup_weights(nc.scalar.copy, scalar_piece, 2 * half)
+            if 0 <= slot + 1 < UNITS:
+                transpose_and_group(slot + 1)
+            if has_piece:
+                regroup_weights(nc.scalar.copy, scalar_piece, 2 * half + 1)
+
+            if slot >= 0:
+                multiply(slot)
+            for a in range(ROW_TILES):
+                if slot == max(UNITS - ROW_TILES + a, COUNTS_SLOT):
+                    divide_and_store(a)

@@ -29,17 +29,13 @@ UNIT_BANKS = UNIT_PASSES // BANK_PASSES
 
 PIECE_PASSES = 4
 PIECES = PASSES // PIECE_PASSES
-VECTOR_PIECES = 2
+SCALAR_PASSES = 3
 
-FIRST_SLOT = -2
+THRESHOLD_LEAD = 2
+TRANSPOSE_LEAD = 1
+MULTIPLY_LAG = 2
 LOAD_LEAD = 6
-COUNTS_SLOT = UNITS - 1 + FIRST_SLOT
-
-
-def piece_slot(h):
-    if h < VECTOR_PIECES:
-        return FIRST_SLOT + h
-    return 2 * h - 5
+FIRST_SLOT = -THRESHOLD_LEAD
 
 
 def tile_flagbagencoder_k_kernel(tc, flags_matrix, emb_weight, out):
@@ -47,10 +43,10 @@ def tile_flagbagencoder_k_kernel(tc, flags_matrix, emb_weight, out):
     with ExitStack() as ctx:
         consts = ctx.enter_context(tc.tile_pool(name="consts", bufs=1))
         flag_pool = ctx.enter_context(tc.tile_pool(name="flags", bufs=LOAD_LEAD + 2))
-        wraw_pool = ctx.enter_context(tc.tile_pool(name="wraw", bufs=5))
+        wraw_pool = ctx.enter_context(tc.tile_pool(name="wraw", bufs=4))
         wgrp_pool = ctx.enter_context(tc.tile_pool(name="wgrp", bufs=2))
         grouped_pool = ctx.enter_context(tc.tile_pool(name="grouped", bufs=2))
-        codes_pool = ctx.enter_context(tc.tile_pool(name="codes", bufs=2))
+        codes_pool = ctx.enter_context(tc.tile_pool(name="codes", bufs=MULTIPLY_LAG + 2))
         result_pool = ctx.enter_context(tc.tile_pool(name="result", bufs=2))
         psum_words = ctx.enter_context(tc.psum_pool(name="words", bufs=UNIT_BANKS))
         psum_sums = ctx.enter_context(tc.psum_pool(name="sums", bufs=1))
@@ -168,43 +164,37 @@ def tile_flagbagencoder_k_kernel(tc, flags_matrix, emb_weight, out):
             nc.scalar.activation(out=result[:], in_=sums[a][:], func=ACT.Copy, scale=inverse_counts[:, a : a + 1])
             nc.sync.dma_start(out=out[a * P : (a + 1) * P, :], in_=result[:])
 
-        for slot in range(FIRST_SLOT - LOAD_LEAD, UNITS):
+        ctx.enter_context(tc.manual_schedule())
+        for slot in range(FIRST_SLOT - LOAD_LEAD, UNITS + MULTIPLY_LAG):
             ahead = slot + LOAD_LEAD
-            if 0 <= ahead - FIRST_SLOT < UNITS:
-                load_flags(ahead - FIRST_SLOT)
-            for h in range(PIECES):
-                if piece_slot(h) == ahead:
-                    load_weights(h)
+            if 0 <= ahead + THRESHOLD_LEAD < UNITS:
+                load_flags(ahead + THRESHOLD_LEAD)
+            if ahead % 2 == 0 and 0 <= (ahead + 2) // 2 < PIECES:
+                load_weights((ahead + 2) // 2)
             if slot < FIRST_SLOT:
                 continue
+            piece, second_slot = divmod(slot + 2, 2)
+            has_piece = piece < PIECES
 
-            if slot >= 0:
-                quantise_mask(slot)
-            if slot - FIRST_SLOT < UNITS:
-                threshold_and_count(slot - FIRST_SLOT)
-            if slot == COUNTS_SLOT:
+            if slot + THRESHOLD_LEAD < UNITS:
+                threshold_and_count(slot + THRESHOLD_LEAD)
+            if slot + THRESHOLD_LEAD == UNITS - 1:
                 invert_counts()
-            for h in range(PIECES):
-                if h < VECTOR_PIECES and piece_slot(h) + 1 == slot:
-                    quantise_weights(h)
-                if h >= VECTOR_PIECES and piece_slot(h) + 2 == slot:
-                    quantise_weights(h)
-            for h in range(VECTOR_PIECES):
-                if piece_slot(h) == slot:
-                    for s in range(PIECE_PASSES):
-                        regroup_weights(nc.vector.tensor_copy, h, s)
+            if has_piece and second_slot:
+                regroup_weights(nc.vector.tensor_copy, piece, SCALAR_PASSES)
+            if not second_slot and 0 <= piece - 1 < PIECES:
+                quantise_weights(piece - 1)
+            if 0 <= slot < UNITS:
+                quantise_mask(slot)
 
-            scalar_piece, half = divmod(slot + 5, 2)
-            has_piece = VECTOR_PIECES <= scalar_piece < PIECES
             if has_piece:
-                regroup_weights(nc.scalar.copy, scalar_piece, 2 * half)
-            if 0 <= slot + 1 < UNITS:
-                transpose_and_group(slot + 1)
-            if has_piece:
-                regroup_weights(nc.scalar.copy, scalar_piece, 2 * half + 1)
+                regroup_weights(nc.scalar.copy, piece, 2 * second_slot)
+            if 0 <= slot + TRANSPOSE_LEAD < UNITS:
+                transpose_and_group(slot + TRANSPOSE_LEAD)
+            if has_piece and not second_slot:
+                regroup_weights(nc.scalar.copy, piece, 1)
 
-            if slot >= 0:
-                multiply(slot)
-            for a in range(ROW_TILES):
-                if slot == max(UNITS - ROW_TILES + a, COUNTS_SLOT):
-                    divide_and_store(a)
+            if 0 <= slot - MULTIPLY_LAG:
+                multiply(slot - MULTIPLY_LAG)
+                if slot - MULTIPLY_LAG >= UNITS - ROW_TILES:
+                    divide_and_store((slot - MULTIPLY_LAG) % ROW_TILES)

@@ -27,11 +27,12 @@ UNITS = ROW_TILES * (K // UNIT_K)
 BANK_PASSES = 2
 UNIT_BANKS = UNIT_PASSES // BANK_PASSES
 
-PIECE_PASSES = 4
+PIECE_PASSES = 2
 PIECES = PASSES // PIECE_PASSES
-SCALAR_PASSES = 3
 
 THRESHOLD_LEAD = 2
+WEIGHT_LEAD = 1
+WEIGHT_BUFFERS = 2
 TRANSPOSE_LEAD = 1
 MULTIPLY_LAG = 2
 LOAD_LEAD = 6
@@ -43,8 +44,8 @@ def tile_flagbagencoder_k_kernel(tc, flags_matrix, emb_weight, out):
     with ExitStack() as ctx:
         consts = ctx.enter_context(tc.tile_pool(name="consts", bufs=1))
         flag_pool = ctx.enter_context(tc.tile_pool(name="flags", bufs=LOAD_LEAD + 2))
-        wraw_pool = ctx.enter_context(tc.tile_pool(name="wraw", bufs=4))
-        wgrp_pool = ctx.enter_context(tc.tile_pool(name="wgrp", bufs=2))
+        wraw_pool = ctx.enter_context(tc.tile_pool(name="wraw", bufs=LOAD_LEAD + 2))
+        wgrp_pool = ctx.enter_context(tc.tile_pool(name="wgrp", bufs=WEIGHT_BUFFERS))
         grouped_pool = ctx.enter_context(tc.tile_pool(name="grouped", bufs=2))
         codes_pool = ctx.enter_context(tc.tile_pool(name="codes", bufs=MULTIPLY_LAG + 2))
         result_pool = ctx.enter_context(tc.tile_pool(name="result", bufs=2))
@@ -119,11 +120,24 @@ def tile_flagbagencoder_k_kernel(tc, flags_matrix, emb_weight, out):
             )
 
         def regroup_weights(copy, h, s):
-            if s == 0:
+            if h not in wgrp_tiles:
                 wgrp_tiles[h] = wgrp_pool.tile([P, PIECE_PASSES, D, PACK], BF16, name="wgrp", align_bytes=64)
-            copy(
+            copy(h, s)
+
+        def regroup_on_scalar(h, s):
+            nc.scalar.copy(
                 out=wgrp_tiles[h][:, s].rearrange("p (c i) j -> p c j i", i=4),
                 in_=wraw_tiles[h][:, s].rearrange("p j (c i) -> p c j i", i=4),
+            )
+
+        def regroup_on_gpsimd(h, s):
+            nc.gpsimd.tensor_scalar(
+                out=wgrp_tiles[h][:, s],
+                in0=wraw_tiles[h][:, s].rearrange("p j d -> p d j"),
+                scalar1=1.0,
+                scalar2=0.0,
+                op0=ALU.mult,
+                op1=ALU.add,
             )
 
         def quantise_weights(h):
@@ -166,33 +180,33 @@ def tile_flagbagencoder_k_kernel(tc, flags_matrix, emb_weight, out):
 
         ctx.enter_context(tc.manual_schedule())
         for slot in range(FIRST_SLOT - LOAD_LEAD, UNITS + MULTIPLY_LAG):
-            ahead = slot + LOAD_LEAD
-            if 0 <= ahead + THRESHOLD_LEAD < UNITS:
-                load_flags(ahead + THRESHOLD_LEAD)
-            if ahead % 2 == 0 and 0 <= (ahead + 2) // 2 < PIECES:
-                load_weights((ahead + 2) // 2)
+            ahead = slot + LOAD_LEAD + THRESHOLD_LEAD
+            if 0 <= ahead < UNITS:
+                load_flags(ahead)
+                load_weights(ahead)
             if slot < FIRST_SLOT:
                 continue
-            piece, second_slot = divmod(slot + 2, 2)
-            has_piece = piece < PIECES
+            coming = slot + THRESHOLD_LEAD
 
-            if slot + THRESHOLD_LEAD < UNITS:
-                threshold_and_count(slot + THRESHOLD_LEAD)
-            if slot + THRESHOLD_LEAD == UNITS - 1:
-                invert_counts()
-            if has_piece and second_slot:
-                regroup_weights(nc.vector.tensor_copy, piece, SCALAR_PASSES)
-            if not second_slot and 0 <= piece - 1 < PIECES:
-                quantise_weights(piece - 1)
             if 0 <= slot < UNITS:
                 quantise_mask(slot)
+            if 0 <= slot + WEIGHT_LEAD < PIECES:
+                quantise_weights(slot + WEIGHT_LEAD)
+            if coming < UNITS:
+                threshold_and_count(coming)
+            if coming == UNITS - 1:
+                invert_counts()
 
-            if has_piece:
-                regroup_weights(nc.scalar.copy, piece, 2 * second_slot)
+            newest = slot + WEIGHT_LEAD + WEIGHT_BUFFERS
+            pieces = range(0 if slot == FIRST_SLOT else newest, min(newest + 1, PIECES))
+
+            for h in pieces:
+                regroup_weights(regroup_on_gpsimd, h, 0)
+
             if 0 <= slot + TRANSPOSE_LEAD < UNITS:
                 transpose_and_group(slot + TRANSPOSE_LEAD)
-            if has_piece and not second_slot:
-                regroup_weights(nc.scalar.copy, piece, 1)
+            for h in pieces:
+                regroup_weights(regroup_on_scalar, h, 1)
 
             if 0 <= slot - MULTIPLY_LAG:
                 multiply(slot - MULTIPLY_LAG)

@@ -29,6 +29,13 @@ UNIT_BANKS = UNIT_PASSES // BANK_PASSES
 
 PIECE_PASSES = 2
 PIECES = PASSES // PIECE_PASSES
+GPSIMD_D = 160
+
+SCALAR_K = 512
+VECTOR_K = UNIT_K - SCALAR_K
+HALF_UNIT_K = UNIT_K // 2
+STEP_SCALE = 2.0**20
+STEP_BIAS = -(2.0**20) * (0.5 + 2.0**-9)
 
 THRESHOLD_LEAD = 2
 WEIGHT_LEAD = 1
@@ -60,7 +67,7 @@ def tile_flagbagencoder_k_kernel(tc, flags_matrix, emb_weight, out):
 
         weight_codes = consts.tile([P, PASSES, D], U32, align_bytes=64)
         weight_scales = consts.tile([P, PASSES, D], U8, align_bytes=64)
-        count_parts = consts.tile([P, UNITS], F32)
+        count_parts = consts.tile([P, 2 * UNITS], F32)
         counts = consts.tile([P, ROW_TILES], F32)
         inverse_counts = consts.tile([P, ROW_TILES], F32)
         sums = [psum_sums.tile([P, D], F32, name="sums%d" % a) for a in range(ROW_TILES)]
@@ -75,7 +82,14 @@ def tile_flagbagencoder_k_kernel(tc, flags_matrix, emb_weight, out):
         def load_flags(i):
             c, a = divmod(i, ROW_TILES)
             flag_tiles[i] = flag_pool.tile([P, UNIT_K], BF16, name="flags")
-            nc.sync.dma_start(out=flag_tiles[i][:], in_=flags_view[c, a])
+            step = HALF_UNIT_K if i == 0 else UNIT_K
+            for first in range(0, UNIT_K, step):
+                nc.sync.dma_start(
+                    out=flag_tiles[i][:, first : first + step], in_=flags_view[c, a, :, first : first + step]
+                )
+
+        def vector_share(i):
+            return HALF_UNIT_K if i == 0 else VECTOR_K
 
         def load_weights(h):
             wraw_tiles[h] = wraw_pool.tile([P, PIECE_PASSES, PACK, D], BF16, name="wraw")
@@ -86,13 +100,23 @@ def tile_flagbagencoder_k_kernel(tc, flags_matrix, emb_weight, out):
 
         def threshold_and_count(i):
             nc.vector.tensor_scalar(
-                out=flag_tiles[i][:],
-                in0=flag_tiles[i][:],
+                out=flag_tiles[i][:, : vector_share(i)],
+                in0=flag_tiles[i][:, : vector_share(i)],
                 scalar1=0.5,
                 scalar2=None,
                 op0=ALU.is_gt,
                 op1=ALU.add,
                 accum_out=count_parts[:, i : i + 1],
+            )
+
+        def threshold_and_count_on_scalar(i):
+            nc.scalar.activation(
+                out=flag_tiles[i][:, vector_share(i) :],
+                in_=flag_tiles[i][:, vector_share(i) :],
+                func=ACT.Sigmoid,
+                scale=STEP_SCALE,
+                bias=STEP_BIAS,
+                accum_out=count_parts[:, UNITS + i : UNITS + i + 1],
             )
 
         def transpose_and_group(i):
@@ -115,30 +139,32 @@ def tile_flagbagencoder_k_kernel(tc, flags_matrix, emb_weight, out):
         def quantise_mask(i):
             mask_codes[i] = codes_pool.tile([P, UNIT_K // PACK], U32, name="mcodes", align_bytes=64)
             mask_scales[i] = codes_pool.tile([P, UNIT_K // PACK], U8, name="mscales", align_bytes=64)
-            nc.vector.quantize_mx(
-                out=mask_codes[i][:].bitcast(FP8X4), scales=mask_scales[i][:], in_=grouped_tiles[i][:]
-            )
+            parts = 2 if i == UNITS - 1 else 1
+            words = UNIT_K // PACK // parts
+            for first in range(0, UNIT_K // PACK, words):
+                nc.vector.quantize_mx(
+                    out=mask_codes[i][:, first : first + words].bitcast(FP8X4),
+                    scales=mask_scales[i][:, first : first + words],
+                    in_=grouped_tiles[i][:, first * PACK : (first + words) * PACK],
+                )
 
-        def regroup_weights(copy, h, s):
-            if h not in wgrp_tiles:
-                wgrp_tiles[h] = wgrp_pool.tile([P, PIECE_PASSES, D, PACK], BF16, name="wgrp", align_bytes=64)
-            copy(h, s)
-
-        def regroup_on_scalar(h, s):
-            nc.scalar.copy(
-                out=wgrp_tiles[h][:, s].rearrange("p (c i) j -> p c j i", i=4),
-                in_=wraw_tiles[h][:, s].rearrange("p j (c i) -> p c j i", i=4),
-            )
-
-        def regroup_on_gpsimd(h, s):
+        def regroup_on_gpsimd(h):
+            wgrp_tiles[h] = wgrp_pool.tile([P, PIECE_PASSES, D, PACK], BF16, name="wgrp", align_bytes=64)
             nc.gpsimd.tensor_scalar(
-                out=wgrp_tiles[h][:, s],
-                in0=wraw_tiles[h][:, s].rearrange("p j d -> p d j"),
+                out=wgrp_tiles[h][:, :, :GPSIMD_D, :],
+                in0=wraw_tiles[h][:, :, :, :GPSIMD_D].rearrange("p s j d -> p s d j"),
                 scalar1=1.0,
                 scalar2=0.0,
                 op0=ALU.mult,
                 op1=ALU.add,
             )
+
+        def regroup_on_scalar(h):
+            for s in range(PIECE_PASSES):
+                nc.scalar.copy(
+                    out=wgrp_tiles[h][:, s, GPSIMD_D:].rearrange("p (c i) j -> p c j i", i=4),
+                    in_=wraw_tiles[h][:, s, :, GPSIMD_D:].rearrange("p j (c i) -> p c j i", i=4),
+                )
 
         def quantise_weights(h):
             piece = slice(h * PIECE_PASSES, (h + 1) * PIECE_PASSES)
@@ -188,25 +214,27 @@ def tile_flagbagencoder_k_kernel(tc, flags_matrix, emb_weight, out):
                 continue
             coming = slot + THRESHOLD_LEAD
 
+            if coming < UNITS:
+                threshold_and_count(coming)
             if 0 <= slot < UNITS:
                 quantise_mask(slot)
             if 0 <= slot + WEIGHT_LEAD < PIECES:
                 quantise_weights(slot + WEIGHT_LEAD)
-            if coming < UNITS:
-                threshold_and_count(coming)
-            if coming == UNITS - 1:
+            if slot == UNITS - ROW_TILES + MULTIPLY_LAG:
                 invert_counts()
 
             newest = slot + WEIGHT_LEAD + WEIGHT_BUFFERS
             pieces = range(0 if slot == FIRST_SLOT else newest, min(newest + 1, PIECES))
 
             for h in pieces:
-                regroup_weights(regroup_on_gpsimd, h, 0)
+                regroup_on_gpsimd(h)
 
             if 0 <= slot + TRANSPOSE_LEAD < UNITS:
                 transpose_and_group(slot + TRANSPOSE_LEAD)
+            if coming < UNITS:
+                threshold_and_count_on_scalar(coming)
             for h in pieces:
-                regroup_weights(regroup_on_scalar, h, 1)
+                regroup_on_scalar(h)
 
             if 0 <= slot - MULTIPLY_LAG:
                 multiply(slot - MULTIPLY_LAG)

@@ -60,7 +60,7 @@ def tile_flagbagencoder_k_kernel(tc, flags_matrix, emb_weight, out):
         psum_sums = ctx.enter_context(tc.psum_pool(name="sums", bufs=1))
 
         flags_view = flags_matrix.rearrange("(a p) (c k) -> c a p k", p=P, k=UNIT_K)
-        weight_view = emb_weight.rearrange("(s u p e) d -> p s u e d", u=2, p=P, e=2)
+        weight_view = emb_weight.rearrange("(s p j) d -> p s j d", p=P, j=PACK)
 
         identity = consts.tile([P, P], F32)
         make_identity(nc, identity[:])
@@ -94,7 +94,7 @@ def tile_flagbagencoder_k_kernel(tc, flags_matrix, emb_weight, out):
         def load_weights(h):
             wraw_tiles[h] = wraw_pool.tile([P, PIECE_PASSES, PACK, D], BF16, name="wraw")
             nc.sync.dma_start(
-                out=wraw_tiles[h][:].rearrange("p s (u e) d -> p s u e d", u=2),
+                out=wraw_tiles[h][:],
                 in_=weight_view[:, h * PIECE_PASSES : (h + 1) * PIECE_PASSES],
             )
 
@@ -129,8 +129,8 @@ def tile_flagbagencoder_k_kernel(tc, flags_matrix, emb_weight, out):
                 bank = psum_words.tile([P, BANK_PASSES, 2, P], F32, name="bank")
                 for g in range(BANK_PASSES):
                     for u in range(2):
-                        first = ((b * BANK_PASSES + g) * 2 + u) * P
-                        nc.tensor.transpose(bank[:, g, u, :], words[:, first : first + P], identity[:])
+                        first = (b * BANK_PASSES + g) * 2 * P
+                        nc.tensor.transpose(bank[:, g, u, :], words[:, first + u : first + 2 * P : 2], identity[:])
                 nc.scalar.copy(
                     out=grouped_words[:, b * BANK_PASSES : (b + 1) * BANK_PASSES],
                     in_=bank[:].rearrange("p g u t -> p g t u"),

@@ -29,22 +29,21 @@ UNIT_BANKS = UNIT_PASSES // BANK_PASSES
 
 PIECE_PASSES = 2
 PIECES = PASSES // PIECE_PASSES
+RANGE_PIECES = UNIT_PASSES // PIECE_PASSES
 GPSIMD_D = 160
 
-SCALAR_K = 512
+SCALAR_K = 448
 VECTOR_K = UNIT_K - SCALAR_K
 HALF_UNIT_K = UNIT_K // 2
+COUNT_PARTS = 2 * UNITS + ROW_TILES
 STEP_SCALE = 2.0**20
 STEP_BIAS = -(2.0**20) * (0.5 + 2.0**-9)
 
-THRESHOLD_LEAD = 2
-WEIGHT_LEAD = 1
+LEAD = 1
 WEIGHT_BUFFERS = 2
-TRANSPOSE_LEAD = 1
-MULTIPLY_LAG = 2
 LOAD_LEAD = 6
-FIRST_SLOT = -THRESHOLD_LEAD
-
+FIRST_SLOT = -LEAD
+CODES_BUFFERS = ROW_TILES + 1
 
 def tile_flagbagencoder_k_kernel(tc, flags_matrix, emb_weight, out):
     nc = tc.nc
@@ -54,7 +53,7 @@ def tile_flagbagencoder_k_kernel(tc, flags_matrix, emb_weight, out):
         wraw_pool = ctx.enter_context(tc.tile_pool(name="wraw", bufs=LOAD_LEAD + 2))
         wgrp_pool = ctx.enter_context(tc.tile_pool(name="wgrp", bufs=WEIGHT_BUFFERS))
         grouped_pool = ctx.enter_context(tc.tile_pool(name="grouped", bufs=2))
-        codes_pool = ctx.enter_context(tc.tile_pool(name="codes", bufs=MULTIPLY_LAG + 2))
+        codes_pool = ctx.enter_context(tc.tile_pool(name="codes", bufs=CODES_BUFFERS))
         result_pool = ctx.enter_context(tc.tile_pool(name="result", bufs=2))
         psum_words = ctx.enter_context(tc.psum_pool(name="words", bufs=UNIT_BANKS))
         psum_sums = ctx.enter_context(tc.psum_pool(name="sums", bufs=1))
@@ -67,7 +66,7 @@ def tile_flagbagencoder_k_kernel(tc, flags_matrix, emb_weight, out):
 
         weight_codes = consts.tile([P, PASSES, D], U32, align_bytes=64)
         weight_scales = consts.tile([P, PASSES, D], U8, align_bytes=64)
-        count_parts = consts.tile([P, 2 * UNITS], F32)
+        count_parts = consts.tile([P, COUNT_PARTS], F32)
         counts = consts.tile([P, ROW_TILES], F32)
         inverse_counts = consts.tile([P, ROW_TILES], F32)
         sums = [psum_sums.tile([P, D], F32, name="sums%d" % a) for a in range(ROW_TILES)]
@@ -88,9 +87,6 @@ def tile_flagbagencoder_k_kernel(tc, flags_matrix, emb_weight, out):
                     out=flag_tiles[i][:, first : first + step], in_=flags_view[c, a, :, first : first + step]
                 )
 
-        def vector_share(i):
-            return HALF_UNIT_K if i == 0 else VECTOR_K
-
         def load_weights(h):
             wraw_tiles[h] = wraw_pool.tile([P, PIECE_PASSES, PACK, D], BF16, name="wraw")
             nc.sync.dma_start(
@@ -99,20 +95,24 @@ def tile_flagbagencoder_k_kernel(tc, flags_matrix, emb_weight, out):
             )
 
         def threshold_and_count(i):
-            nc.vector.tensor_scalar(
-                out=flag_tiles[i][:, : vector_share(i)],
-                in0=flag_tiles[i][:, : vector_share(i)],
-                scalar1=0.5,
-                scalar2=None,
-                op0=ALU.is_gt,
-                op1=ALU.add,
-                accum_out=count_parts[:, i : i + 1],
-            )
+            bounds = (0, HALF_UNIT_K, VECTOR_K) if i == 0 else (0, VECTOR_K)
+            for part in range(len(bounds) - 1):
+                mask = flag_tiles[i][:, bounds[part] : bounds[part + 1]]
+                column = i + part * 2 * UNITS
+                nc.vector.tensor_scalar(
+                    out=mask,
+                    in0=mask,
+                    scalar1=0.5,
+                    scalar2=None,
+                    op0=ALU.is_gt,
+                    op1=ALU.add,
+                    accum_out=count_parts[:, column : column + 1],
+                )
 
         def threshold_and_count_on_scalar(i):
             nc.scalar.activation(
-                out=flag_tiles[i][:, vector_share(i) :],
-                in_=flag_tiles[i][:, vector_share(i) :],
+                out=flag_tiles[i][:, VECTOR_K:],
+                in_=flag_tiles[i][:, VECTOR_K:],
                 func=ACT.Sigmoid,
                 scale=STEP_SCALE,
                 bias=STEP_BIAS,
@@ -174,10 +174,10 @@ def tile_flagbagencoder_k_kernel(tc, flags_matrix, emb_weight, out):
                 in_=wgrp_tiles[h][:].rearrange("p s d j -> p (s d j)"),
             )
 
-        def multiply(i):
+        def multiply(i, h):
             c, a = divmod(i, ROW_TILES)
-            for g in range(UNIT_PASSES):
-                s = c * UNIT_PASSES + g
+            for s in range(h * PIECE_PASSES, (h + 1) * PIECE_PASSES):
+                g = s - c * UNIT_PASSES
                 rows = slice(g * P, (g + 1) * P)
                 nc.tensor.matmul_mx(
                     out=sums[a][:],
@@ -205,38 +205,37 @@ def tile_flagbagencoder_k_kernel(tc, flags_matrix, emb_weight, out):
             nc.sync.dma_start(out=out[a * P : (a + 1) * P, :], in_=result[:])
 
         ctx.enter_context(tc.manual_schedule())
-        for slot in range(FIRST_SLOT - LOAD_LEAD, UNITS + MULTIPLY_LAG):
-            ahead = slot + LOAD_LEAD + THRESHOLD_LEAD
-            if 0 <= ahead < UNITS:
+        nc.gpsimd.memset(count_parts[:, 2 * UNITS :], 0.0)
+        for slot in range(FIRST_SLOT - LOAD_LEAD, UNITS + 1):
+            ahead = slot + LEAD + LOAD_LEAD
+            if ahead < UNITS:
                 load_flags(ahead)
                 load_weights(ahead)
             if slot < FIRST_SLOT:
                 continue
-            coming = slot + THRESHOLD_LEAD
+            coming = slot + LEAD
 
             if coming < UNITS:
                 threshold_and_count(coming)
+            if slot == UNITS - 1:
+                quantise_weights(slot)
+                invert_counts()
             if 0 <= slot < UNITS:
                 quantise_mask(slot)
-            if 0 <= slot + WEIGHT_LEAD < PIECES:
-                quantise_weights(slot + WEIGHT_LEAD)
-            if slot == UNITS - ROW_TILES + MULTIPLY_LAG:
-                invert_counts()
+            if 0 <= slot < UNITS - 1:
+                quantise_weights(slot)
 
-            newest = slot + WEIGHT_LEAD + WEIGHT_BUFFERS
-            pieces = range(0 if slot == FIRST_SLOT else newest, min(newest + 1, PIECES))
-
-            for h in pieces:
-                regroup_on_gpsimd(h)
-
-            if 0 <= slot + TRANSPOSE_LEAD < UNITS:
-                transpose_and_group(slot + TRANSPOSE_LEAD)
             if coming < UNITS:
+                regroup_on_gpsimd(coming)
                 threshold_and_count_on_scalar(coming)
-            for h in pieces:
-                regroup_on_scalar(h)
+                regroup_on_scalar(coming)
+                transpose_and_group(coming)
 
-            if 0 <= slot - MULTIPLY_LAG:
-                multiply(slot - MULTIPLY_LAG)
-                if slot - MULTIPLY_LAG >= UNITS - ROW_TILES:
-                    divide_and_store((slot - MULTIPLY_LAG) % ROW_TILES)
+            for i in range(UNITS):
+                c, a = divmod(i, ROW_TILES)
+                last_piece = (c + 1) * RANGE_PIECES - 1
+                for h in range(c * RANGE_PIECES, last_piece + 1):
+                    if max(i + 1, h) == slot:
+                        multiply(i, h)
+                if last_piece == PIECES - 1 and max(i + 1, last_piece) == slot:
+                    divide_and_store(a)

@@ -32,7 +32,7 @@ PIECES = PASSES // PIECE_PASSES
 RANGE_PIECES = UNIT_PASSES // PIECE_PASSES
 GPSIMD_D = 160
 
-SCALAR_K = 448
+SCALAR_K = 640
 VECTOR_K = UNIT_K - SCALAR_K
 HALF_UNIT_K = UNIT_K // 2
 COUNT_PARTS = 2 * UNITS + ROW_TILES
@@ -40,6 +40,7 @@ STEP_SCALE = 2.0**20
 STEP_BIAS = -(2.0**20) * (0.5 + 2.0**-9)
 
 LEAD = 1
+VECTOR_DIVIDES = ROW_TILES - 2
 WEIGHT_BUFFERS = 2
 LOAD_LEAD = 6
 FIRST_SLOT = -LEAD
@@ -54,7 +55,7 @@ def tile_flagbagencoder_k_kernel(tc, flags_matrix, emb_weight, out):
         wgrp_pool = ctx.enter_context(tc.tile_pool(name="wgrp", bufs=WEIGHT_BUFFERS))
         grouped_pool = ctx.enter_context(tc.tile_pool(name="grouped", bufs=2))
         codes_pool = ctx.enter_context(tc.tile_pool(name="codes", bufs=CODES_BUFFERS))
-        result_pool = ctx.enter_context(tc.tile_pool(name="result", bufs=2))
+        result_pool = ctx.enter_context(tc.tile_pool(name="result", bufs=ROW_TILES))
         psum_words = ctx.enter_context(tc.psum_pool(name="words", bufs=UNIT_BANKS))
         psum_sums = ctx.enter_context(tc.psum_pool(name="sums", bufs=1))
 
@@ -201,7 +202,11 @@ def tile_flagbagencoder_k_kernel(tc, flags_matrix, emb_weight, out):
 
         def divide_and_store(a):
             result = result_pool.tile([P, D], F32, name="result")
-            nc.scalar.activation(out=result[:], in_=sums[a][:], func=ACT.Copy, scale=inverse_counts[:, a : a + 1])
+            factor = inverse_counts[:, a : a + 1]
+            if a == VECTOR_DIVIDES:
+                nc.vector.tensor_scalar(out=result[:], in0=sums[a][:], scalar1=factor, scalar2=None, op0=ALU.mult)
+            else:
+                nc.scalar.activation(out=result[:], in_=sums[a][:], func=ACT.Copy, scale=factor)
             nc.sync.dma_start(out=out[a * P : (a + 1) * P, :], in_=result[:])
 
         ctx.enter_context(tc.manual_schedule())
@@ -210,7 +215,9 @@ def tile_flagbagencoder_k_kernel(tc, flags_matrix, emb_weight, out):
             ahead = slot + LEAD + LOAD_LEAD
             if ahead < UNITS:
                 load_flags(ahead)
-                load_weights(ahead)
+            for h in ((), (0, 1))[ahead] if ahead < 2 else (ahead,):
+                if h < PIECES:
+                    load_weights(h)
             if slot < FIRST_SLOT:
                 continue
             coming = slot + LEAD
@@ -228,8 +235,11 @@ def tile_flagbagencoder_k_kernel(tc, flags_matrix, emb_weight, out):
             if coming < UNITS:
                 regroup_on_gpsimd(coming)
                 threshold_and_count_on_scalar(coming)
-                regroup_on_scalar(coming)
+                if slot > FIRST_SLOT:
+                    regroup_on_scalar(coming)
                 transpose_and_group(coming)
+                if slot == FIRST_SLOT:
+                    regroup_on_scalar(coming)
 
             for i in range(UNITS):
                 c, a = divmod(i, ROW_TILES)

@@ -60,7 +60,7 @@ def tile_flagbagencoder_k_kernel(tc, flags_matrix, emb_weight, out):
         psum_sums = ctx.enter_context(tc.psum_pool(name="sums", bufs=1))
 
         flags_view = flags_matrix.rearrange("(a p) (c k) -> c a p k", p=P, k=UNIT_K)
-        weight_view = emb_weight.rearrange("(s p j) d -> p s j d", p=P, j=PACK)
+        weight_view = emb_weight.rearrange("(s u p e) d -> p s u e d", u=2, p=P, e=2)
 
         identity = consts.tile([P, P], F32)
         make_identity(nc, identity[:])
@@ -91,7 +91,7 @@ def tile_flagbagencoder_k_kernel(tc, flags_matrix, emb_weight, out):
         def load_weights(h):
             wraw_tiles[h] = wraw_pool.tile([P, PIECE_PASSES, PACK, D], BF16, name="wraw")
             nc.sync.dma_start(
-                out=wraw_tiles[h][:],
+                out=wraw_tiles[h][:].rearrange("p s (u e) d -> p s u e d", u=2),
                 in_=weight_view[:, h * PIECE_PASSES : (h + 1) * PIECE_PASSES],
             )
 
@@ -130,8 +130,8 @@ def tile_flagbagencoder_k_kernel(tc, flags_matrix, emb_weight, out):
                 bank = psum_words.tile([P, BANK_PASSES, 2, P], F32, name="bank")
                 for g in range(BANK_PASSES):
                     for u in range(2):
-                        first = (b * BANK_PASSES + g) * 2 * P
-                        nc.tensor.transpose(bank[:, g, u, :], words[:, first + u : first + 2 * P : 2], identity[:])
+                        first = ((b * BANK_PASSES + g) * 2 + u) * P
+                        nc.tensor.transpose(bank[:, g, u, :], words[:, first : first + P], identity[:])
                 nc.scalar.copy(
                     out=grouped_words[:, b * BANK_PASSES : (b + 1) * BANK_PASSES],
                     in_=bank[:].rearrange("p g u t -> p g t u"),

@@ -32,7 +32,7 @@ PIECES = PASSES // PIECE_PASSES
 RANGE_PIECES = UNIT_PASSES // PIECE_PASSES
 GPSIMD_D = 160
 
-SCALAR_K = 640
+SCALAR_K = 512
 VECTOR_K = UNIT_K - SCALAR_K
 HALF_UNIT_K = UNIT_K // 2
 COUNT_PARTS = 2 * UNITS + ROW_TILES
@@ -40,6 +40,7 @@ STEP_SCALE = 2.0**20
 STEP_BIAS = -(2.0**20) * (0.5 + 2.0**-9)
 
 LEAD = 1
+PAIRS_PER_SLOT = RANGE_PIECES
 VECTOR_DIVIDES = ROW_TILES - 2
 WEIGHT_BUFFERS = 2
 LOAD_LEAD = 6
@@ -210,6 +211,7 @@ def tile_flagbagencoder_k_kernel(tc, flags_matrix, emb_weight, out):
             nc.sync.dma_start(out=out[a * P : (a + 1) * P, :], in_=result[:])
 
         ctx.enter_context(tc.manual_schedule())
+        waiting = []
         nc.gpsimd.memset(count_parts[:, 2 * UNITS :], 0.0)
         for slot in range(FIRST_SLOT - LOAD_LEAD, UNITS + 1):
             ahead = slot + LEAD + LOAD_LEAD
@@ -242,10 +244,13 @@ def tile_flagbagencoder_k_kernel(tc, flags_matrix, emb_weight, out):
                     regroup_on_scalar(coming)
 
             for i in range(UNITS):
-                c, a = divmod(i, ROW_TILES)
-                last_piece = (c + 1) * RANGE_PIECES - 1
-                for h in range(c * RANGE_PIECES, last_piece + 1):
+                c = i // ROW_TILES
+                for h in range(c * RANGE_PIECES, (c + 1) * RANGE_PIECES):
                     if max(i + 1, h) == slot:
-                        multiply(i, h)
-                if last_piece == PIECES - 1 and max(i + 1, last_piece) == slot:
-                    divide_and_store(a)
+                        waiting.append((i, h))
+            now = len(waiting) if slot >= UNITS - 1 else min(len(waiting), PAIRS_PER_SLOT)
+            for i, h in waiting[:now]:
+                multiply(i, h)
+                if h == PIECES - 1:
+                    divide_and_store(i % ROW_TILES)
+            waiting = waiting[now:]

from contextlib import ExitStack

import concourse.mybir as mybir
from concourse.masks import make_identity

BF16 = mybir.dt.bfloat16
F32 = mybir.dt.float32
U32 = mybir.dt.uint32
U8 = mybir.dt.uint8
FP8X4 = mybir.dt.float8_e4m3fn_x4
ALU = mybir.AluOpType
AX = mybir.AxisListType
ACT = mybir.ActivationFunctionType

T, K, D = 512, 16384, 256
FLOPS = 2 * T * K * D

P = 128
PACK = 4
K_PASS = P * PACK
PASSES = K // K_PASS
ROW_TILES = T // P

UNIT_K = 4096
UNIT_PASSES = UNIT_K // K_PASS
UNITS = ROW_TILES * (K // UNIT_K)
BANK_PASSES = 2
UNIT_BANKS = UNIT_PASSES // BANK_PASSES

PIECE_PASSES = 2
PIECES = PASSES // PIECE_PASSES
RANGE_PIECES = UNIT_PASSES // PIECE_PASSES
GPSIMD_D = 160

SCALAR_K = 512
VECTOR_K = UNIT_K - SCALAR_K
HALF_UNIT_K = UNIT_K // 2
COUNT_PARTS = 2 * UNITS + ROW_TILES
STEP_SCALE = 2.0**20
STEP_BIAS = -(2.0**20) * (0.5 + 2.0**-9)

LEAD = 1
PAIRS_PER_SLOT = RANGE_PIECES
VECTOR_DIVIDES = ROW_TILES - 2
WEIGHT_BUFFERS = 2
LOAD_LEAD = 6
FIRST_SLOT = -LEAD
CODES_BUFFERS = ROW_TILES + 1

def tile_flagbagencoder_k_kernel(tc, flags_matrix, emb_weight, out):
    nc = tc.nc
    with ExitStack() as ctx:
        consts = ctx.enter_context(tc.tile_pool(name="consts", bufs=1))
        flag_pool = ctx.enter_context(tc.tile_pool(name="flags", bufs=LOAD_LEAD + 2))
        wraw_pool = ctx.enter_context(tc.tile_pool(name="wraw", bufs=LOAD_LEAD + 2))
        wgrp_pool = ctx.enter_context(tc.tile_pool(name="wgrp", bufs=WEIGHT_BUFFERS))
        grouped_pool = ctx.enter_context(tc.tile_pool(name="grouped", bufs=2))
        codes_pool = ctx.enter_context(tc.tile_pool(name="codes", bufs=CODES_BUFFERS))
        result_pool = ctx.enter_context(tc.tile_pool(name="result", bufs=ROW_TILES))
        psum_words = ctx.enter_context(tc.psum_pool(name="words", bufs=UNIT_BANKS))
        psum_sums = ctx.enter_context(tc.psum_pool(name="sums", bufs=1))

        flags_view = flags_matrix.rearrange("(a p) (c k) -> c a p k", p=P, k=UNIT_K)
        weight_view = emb_weight.rearrange("(s u p e) d -> p s u e d", u=2, p=P, e=2)

        identity = consts.tile([P, P], F32)
        make_identity(nc, identity[:])

        weight_codes = consts.tile([P, PASSES, D], U32, align_bytes=64)
        weight_scales = consts.tile([P, PASSES, D], U8, align_bytes=64)
        count_parts = consts.tile([P, COUNT_PARTS], F32)
        counts = consts.tile([P, ROW_TILES], F32)
        inverse_counts = consts.tile([P, ROW_TILES], F32)
        sums = [psum_sums.tile([P, D], F32, name="sums%d" % a) for a in range(ROW_TILES)]

        flag_tiles = {}
        wraw_tiles = {}
        wgrp_tiles = {}
        grouped_tiles = {}
        mask_codes = {}
        mask_scales = {}

        def load_flags(i):
            c, a = divmod(i, ROW_TILES)
            flag_tiles[i] = flag_pool.tile([P, UNIT_K], BF16, name="flags")
            step = HALF_UNIT_K if i == 0 else UNIT_K
            for first in range(0, UNIT_K, step):
                nc.sync.dma_start(
                    out=flag_tiles[i][:, first : first + step], in_=flags_view[c, a, :, first : first + step]
                )

        def load_weights(h):
            wraw_tiles[h] = wraw_pool.tile([P, PIECE_PASSES, PACK, D], BF16, name="wraw")
            nc.sync.dma_start(
                out=wraw_tiles[h][:].rearrange("p s (u e) d -> p s u e d", u=2),
                in_=weight_view[:, h * PIECE_PASSES : (h + 1) * PIECE_PASSES],
            )

        def threshold_and_count(i):
            bounds = (0, HALF_UNIT_K, VECTOR_K) if i == 0 else (0, VECTOR_K)
            for part in range(len(bounds) - 1):
                mask = flag_tiles[i][:, bounds[part] : bounds[part + 1]]
                column = i + part * 2 * UNITS
                nc.vector.tensor_scalar(
                    out=mask,
                    in0=mask,
                    scalar1=0.5,
                    scalar2=None,
                    op0=ALU.is_gt,
                    op1=ALU.add,
                    accum_out=count_parts[:, column : column + 1],
                )

        def threshold_and_count_on_scalar(i):
            nc.scalar.activation(
                out=flag_tiles[i][:, VECTOR_K:],
                in_=flag_tiles[i][:, VECTOR_K:],
                func=ACT.Sigmoid,
                scale=STEP_SCALE,
                bias=STEP_BIAS,
                accum_out=count_parts[:, UNITS + i : UNITS + i + 1],
            )

        def transpose_and_group(i):
            words = flag_tiles[i][:].bitcast(F32)
            grouped_tiles[i] = grouped_pool.tile([P, UNIT_K], BF16, name="grouped", align_bytes=64)
            grouped_words = (
                grouped_tiles[i][:].bitcast(F32).rearrange("p (g t u) -> p g t u", g=UNIT_PASSES, u=2)
            )
            for b in range(UNIT_BANKS):
                bank = psum_words.tile([P, BANK_PASSES, 2, P], F32, name="bank")
                for g in range(BANK_PASSES):
                    for u in range(2):
                        first = ((b * BANK_PASSES + g) * 2 + u) * P
                        nc.tensor.transpose(bank[:, g, u, :], words[:, first : first + P], identity[:])
                nc.scalar.copy(
                    out=grouped_words[:, b * BANK_PASSES : (b + 1) * BANK_PASSES],
                    in_=bank[:].rearrange("p g u t -> p g t u"),
                )

        def quantise_mask(i):
            mask_codes[i] = codes_pool.tile([P, UNIT_K // PACK], U32, name="mcodes", align_bytes=64)
            mask_scales[i] = codes_pool.tile([P, UNIT_K // PACK], U8, name="mscales", align_bytes=64)
            parts = 2 if i == UNITS - 1 else 1
            words = UNIT_K // PACK // parts
            for first in range(0, UNIT_K // PACK, words):
                nc.vector.quantize_mx(
                    out=mask_codes[i][:, first : first + words].bitcast(FP8X4),
                    scales=mask_scales[i][:, first : first + words],
                    in_=grouped_tiles[i][:, first * PACK : (first + words) * PACK],
                )

        def regroup_on_gpsimd(h):
            wgrp_tiles[h] = wgrp_pool.tile([P, PIECE_PASSES, D, PACK], BF16, name="wgrp", align_bytes=64)
            nc.gpsimd.tensor_scalar(
                out=wgrp_tiles[h][:, :, :GPSIMD_D, :],
                in0=wraw_tiles[h][:, :, :, :GPSIMD_D].rearrange("p s j d -> p s d j"),
                scalar1=1.0,
                scalar2=0.0,
                op0=ALU.mult,
                op1=ALU.add,
            )

        def regroup_on_scalar(h):
            for s in range(PIECE_PASSES):
                nc.scalar.copy(
                    out=wgrp_tiles[h][:, s, GPSIMD_D:].rearrange("p (c i) j -> p c j i", i=4),
                    in_=wraw_tiles[h][:, s, :, GPSIMD_D:].rearrange("p j (c i) -> p c j i", i=4),
                )

        def quantise_weights(h):
            piece = slice(h * PIECE_PASSES, (h + 1) * PIECE_PASSES)
            nc.vector.quantize_mx(
                out=weight_codes[:, piece, :].rearrange("p s d -> p (s d)").bitcast(FP8X4),
                scales=weight_scales[:, piece, :].rearrange("p s d -> p (s d)"),
                in_=wgrp_tiles[h][:].rearrange("p s d j -> p (s d j)"),
            )

        def multiply(i, h):
            c, a = divmod(i, ROW_TILES)
            for s in range(h * PIECE_PASSES, (h + 1) * PIECE_PASSES):
                g = s - c * UNIT_PASSES
                rows = slice(g * P, (g + 1) * P)
                nc.tensor.matmul_mx(
                    out=sums[a][:],
                    lhsT=mask_codes[i][:, rows].bitcast(FP8X4),
                    lhsT_scale=mask_scales[i][:, rows],
                    rhs=weight_codes[:, s, :].bitcast(FP8X4),
                    rhs_scale=weight_scales[:, s, :],
                    start=(s == 0),
                    stop=(s == PASSES - 1),
                )

        def invert_counts():
            nc.vector.tensor_reduce(
                out=counts[:],
                in_=count_parts[:].rearrange("p (c a) -> p a c", a=ROW_TILES),
                axis=AX.X,
                op=ALU.add,
            )
            nc.vector.tensor_scalar_max(out=counts[:], in0=counts[:], scalar1=1.0)
            nc.vector.reciprocal(out=inverse_counts[:], in_=counts[:])

        def divide_and_store(a):
            result = result_pool.tile([P, D], F32, name="result")
            factor = inverse_counts[:, a : a + 1]
            if a == VECTOR_DIVIDES:
                nc.vector.tensor_scalar(out=result[:], in0=sums[a][:], scalar1=factor, scalar2=None, op0=ALU.mult)
            else:
                nc.scalar.activation(out=result[:], in_=sums[a][:], func=ACT.Copy, scale=factor)
            nc.sync.dma_start(out=out[a * P : (a + 1) * P, :], in_=result[:])

        ctx.enter_context(tc.manual_schedule())
        waiting = []
        nc.gpsimd.memset(count_parts[:, 2 * UNITS :], 0.0)
        for slot in range(FIRST_SLOT - LOAD_LEAD, UNITS + 1):
            ahead = slot + LEAD + LOAD_LEAD
            if ahead < UNITS:
                load_flags(ahead)
            for h in ((), (0, 1))[ahead] if ahead < 2 else (ahead,):
                if h < PIECES:
                    load_weights(h)
            if slot < FIRST_SLOT:
                continue
            coming = slot + LEAD

            if coming < UNITS:
                threshold_and_count(coming)
            if slot == UNITS - 1:
                quantise_weights(slot)
                invert_counts()
            if 0 <= slot < UNITS:
                quantise_mask(slot)
            if 0 <= slot < UNITS - 1:
                quantise_weights(slot)

            if coming < UNITS:
                regroup_on_gpsimd(coming)
                threshold_and_count_on_scalar(coming)
                if slot > FIRST_SLOT:
                    regroup_on_scalar(coming)
                transpose_and_group(coming)
                if slot == FIRST_SLOT:
                    regroup_on_scalar(coming)

            for i in range(UNITS):
                c = i // ROW_TILES
                for h in range(c * RANGE_PIECES, (c + 1) * RANGE_PIECES):
                    if max(i + 1, h) == slot:
                        waiting.append((i, h))
            now = len(waiting) if slot >= UNITS - 1 else min(len(waiting), PAIRS_PER_SLOT)
            for i, h in waiting[:now]:
                multiply(i, h)
                if h == PIECES - 1:
                    divide_and_store(i % ROW_TILES)
            waiting = waiting[now:]
